import numpy as np
import ml_dtypes


def mxq(x, axis, fmt="e4m3"):
    dtype, down = {"e4m3": (ml_dtypes.float8_e4m3fn, 7), "e5m2": (ml_dtypes.float8_e5m2, 14)}[fmt]
    v = np.moveaxis(np.asarray(x, np.float32).astype(ml_dtypes.bfloat16).astype(np.float64), axis, -1)
    blocks = v.reshape(v.shape[:-1] + (-1, 32))
    amax = np.abs(blocks).max(-1, keepdims=True)
    byte = np.maximum(np.where(amax > 0, np.frexp(amax)[1] - 1 + 127, 0) - down, 1)
    scale = np.exp2(byte - 127.0)
    codes = (blocks / scale).astype(np.float32).astype(dtype).astype(np.float64)
    return np.moveaxis((codes * scale).reshape(v.shape), -1, axis)


WIDE = False


def mx_kscale(k):
    if not WIDE:
        return np.ones(k)
    levels = np.array([10, -10, 5, -5, 0])
    if k % 512:
        return np.exp2(np.random.permutation(np.resize(levels, k // 32))).repeat(32)
    a = np.empty((k // 512, 16))
    for p in range(k // 512):
        a[p, :8] = np.random.permutation(np.resize(levels, 8))
        for g in range(8):
            far = levels[np.abs(levels - a[p, g]) >= 10]
            a[p, g + 8] = far[np.random.randint(len(far))]
    return np.exp2(a.ravel()).repeat(32)


BF16 = ml_dtypes.bfloat16


def bf(x):
    return np.asarray(x, np.float32).astype(BF16)


def f64(x):
    return np.asarray(x).astype(np.float64)


G, S, M, H, E, C = 4, 1024, 512, 512, 16, 64


def setup_inputs():
    t = mx_kscale(H)
    u = mx_kscale(E * C).reshape(E, C)
    return {"h": bf(np.maximum(np.random.standard_normal((E, G, C, H)), 0.0) * 1.4 * t * u[:, None, :, None]),
            "wo": bf(np.random.standard_normal((E, H, M)) * 10.0 / np.sqrt(H * E * C) / t[None, :, None]),
            "combined_weights": bf(np.random.standard_normal((G, S, E, C)) * 0.1 / u)}


def reference(h, wo, combined_weights):
    eo = mxq(f64(h).reshape(E, G * C, H), 2, "e4m3") @ mxq(f64(wo), 1, "e4m3")
    expert_outputs = eo.reshape(E, G, C, M).transpose(1, 0, 2, 3)
    cw = mxq(f64(combined_weights).reshape(G, S, E * C), 2, "e4m3")
    return cw @ mxq(expert_outputs.reshape(G, E * C, M), 1, "e4m3")

@@ -1,0 +1,212 @@
+from contextlib import ExitStack
+
+from concourse import mybir
+from concourse.masks import make_identity
+
+BF16 = mybir.dt.bfloat16
+F32 = mybir.dt.float32
+U32 = mybir.dt.uint32
+U8 = mybir.dt.uint8
+FP8X4 = mybir.dt.float8_e4m3fn_x4
+
+E, G, C, H, M, S = 16, 4, 64, 512, 512, 1024
+P = 128
+PACK = 4
+K_PASS = P * PACK
+K2 = E * C
+HALVES = K2 // K_PASS
+E_HALF = E // HALVES
+S_TILES = S // P
+M_CHUNKS = M // P
+TILES_PER_LOAD = 2
+LOADS_PER_GROUP = S_TILES // TILES_PER_LOAD
+
+FLOPS = 2 * E * G * C * H * M + 2 * G * S * K2 * M
+
+
+def tile_flaxpositionwisemoelayer_pb_t_kernel(tc, h, wo, combined_weights, out):
+    nc = tc.nc
+    with ExitStack() as ctx:
+        const = ctx.enter_context(tc.tile_pool(name="const", bufs=1))
+        keep = ctx.enter_context(tc.tile_pool(name="keep", bufs=1))
+        raw = ctx.enter_context(tc.tile_pool(name="raw", bufs=5))
+        grouped = ctx.enter_context(tc.tile_pool(name="grouped", bufs=2))
+        codes = ctx.enter_context(tc.tile_pool(name="codes", bufs=3))
+        result = ctx.enter_context(tc.tile_pool(name="result", bufs=6))
+        banks = ctx.enter_context(tc.psum_pool(name="banks", bufs=8))
+        ctx.enter_context(tc.manual_schedule())
+
+        ident = const.tile([P, P], F32)
+        make_identity(nc, ident[:])
+
+        cw_codes = keep.tile([P, G, S_TILES, HALVES * P], U32, align_bytes=64)
+        cw_scales = keep.tile([P, G, S_TILES, HALVES * P], U8, align_bytes=64)
+        eo_codes = keep.tile([P, G, HALVES, M], U32, align_bytes=64)
+        eo_scales = keep.tile([P, G, HALVES, M], U8, align_bytes=64)
+        eo_turned = [keep.tile([P, M_CHUNKS, 2, G, E_HALF * C // 2], BF16, name="eo_turned%d" % a) for a in range(HALVES)]
+
+        loaded = {}
+        ready = {}
+
+        def load(e):
+            h_raw = raw.tile([P, 2 * H], BF16)
+            nc.sync.dma_start(out=h_raw[:], in_=h[e].rearrange("g (d n) k -> (g d) (n k)", n=2))
+            wo_raw = raw.tile([P, PACK, M], BF16)
+            nc.sync.dma_start(out=wo_raw[:], in_=wo[e].rearrange("(p t) m -> p t m", t=PACK))
+            g, first = e // LOADS_PER_GROUP, (e % LOADS_PER_GROUP) * TILES_PER_LOAD
+            cw_raw = raw.tile([P, TILES_PER_LOAD, K2], BF16)
+            nc.sync.dma_start(
+                out=cw_raw[:],
+                in_=combined_weights[g].rearrange("(r n) e c -> r n (e c)", n=S_TILES)[:, first : first + TILES_PER_LOAD, :],
+            )
+            loaded[e] = (h_raw, wo_raw, cw_raw)
+
+        def turn_h(e):
+            words = loaded[e][0][:].bitcast(F32)
+            flip = banks.tile([P, 4, P], F32, tag="bank", name="h_flip")
+            for n in range(2):
+                for k in range(2):
+                    nc.tensor.transpose(flip[:, 2 * n + k, :], words[:, n * (H // 2) + k : (n + 1) * (H // 2) : 2], ident[:])
+            h_grouped = grouped.tile([P, G * C * PACK], BF16, align_bytes=64, name="h_grouped")
+            nc.scalar.copy(
+                out=h_grouped[:].bitcast(F32).rearrange("p (u q s) -> p u q s", u=2, s=4),
+                in_=flip[:].rearrange("p s (q u) -> p u q s", u=2),
+            )
+            ready["h", e] = h_grouped
+
+        def turn_cw(e):
+            cw_grouped = grouped.tile([P, TILES_PER_LOAD, HALVES, P, PACK], BF16, align_bytes=64, name="cw_grouped")
+            for j in range(TILES_PER_LOAD):
+                words = loaded[e][2][:, j, :].bitcast(F32)
+                flip = banks.tile([P, HALVES, 2, P], F32, tag="bank", name="cw_flip")
+                for a in range(HALVES):
+                    for k in range(2):
+                        first = a * (K_PASS // 2)
+                        nc.tensor.transpose(flip[:, a, k, :], words[:, first + k : first + K_PASS // 2 : 2], ident[:])
+                nc.scalar.copy(
+                    out=cw_grouped[:, j].rearrange("p a r t -> p (a r t)").bitcast(F32).rearrange("p (a r k) -> p a r k", a=HALVES, k=2),
+                    in_=flip[:].rearrange("p a k r -> p a r k"),
+                )
+            ready["cw", e] = cw_grouped
+
+        def group_wo(e):
+            wo_grouped = grouped.tile([P, M, PACK], BF16, align_bytes=64, name="wo_grouped")
+            nc.vector.tensor_copy(
+                out=wo_grouped[:].rearrange("p (c i) t -> p c t i", i=4),
+                in_=loaded[e][1][:].rearrange("p t (c i) -> p c t i", i=4),
+            )
+            ready["wo", e] = wo_grouped
+
+        def quantise_h(e):
+            h_codes = codes.tile([P, G * C], U32, align_bytes=64)
+            h_scales = codes.tile([P, G * C], U8, align_bytes=64)
+            nc.vector.quantize_mx(out=h_codes[:].bitcast(FP8X4), scales=h_scales[:], in_=ready["h", e][:])
+            ready["h", e] = (h_codes, h_scales)
+
+        def quantise_wo(e):
+            wo_codes = codes.tile([P, M], U32, align_bytes=64)
+            wo_scales = codes.tile([P, M], U8, align_bytes=64)
+            nc.vector.quantize_mx(
+                out=wo_codes[:].bitcast(FP8X4),
+                scales=wo_scales[:],
+                in_=ready["wo", e][:].rearrange("p m t -> p (m t)"),
+            )
+            ready["wo", e] = (wo_codes, wo_scales)
+
+        def quantise_cw(e):
+            g, first = e // LOADS_PER_GROUP, (e % LOADS_PER_GROUP) * TILES_PER_LOAD
+            nc.vector.quantize_mx(
+                out=cw_codes[:, g, first : first + TILES_PER_LOAD, :].rearrange("p j w -> p (j w)").bitcast(FP8X4),
+                scales=cw_scales[:, g, first : first + TILES_PER_LOAD, :].rearrange("p j w -> p (j w)"),
+                in_=ready["cw", e][:].rearrange("p j a r t -> p (j a r t)"),
+            )
+
+        def expert_product(e, engines):
+            a, e_in = e // E_HALF, e % E_HALF
+            h_codes, h_scales = ready["h", e]
+            wo_codes, wo_scales = ready["wo", e]
+            for pair in range(M_CHUNKS // 2):
+                eo_sum = banks.tile([P, 2, G * C], F32, tag="bank", name="eo_sum")
+                for i in range(2):
+                    cols = slice((2 * pair + i) * P, (2 * pair + i + 1) * P)
+                    nc.tensor.matmul_mx(
+                        out=eo_sum[:, i, :],
+                        lhsT=wo_codes[:, cols].bitcast(FP8X4),
+                        lhsT_scale=wo_scales[:, cols],
+                        rhs=h_codes[:].bitcast(FP8X4),
+                        rhs_scale=h_scales[:],
+                        start=True,
+                        stop=True,
+                    )
+                engines[pair](
+                    out=eo_turned[a][:, 2 * pair : 2 * pair + 2, :, :, e_in * C // 2 : (e_in + 1) * C // 2].rearrange("p c u g w -> p (c u g) w"),
+                    in_=eo_sum[:].rearrange("p c (x w) -> p (c x) w", w=C // 2),
+                )
+
+        def turn_eo(a, g, pair, copy):
+            if pair == 0:
+                ready["eo", a, g] = grouped.tile([P, M_CHUNKS, P, PACK], BF16, align_bytes=64, name="eo_grouped")
+            eo_grouped = ready["eo", a, g]
+            flip = banks.tile([P, 2, 2, P], F32, tag="bank", name="eo_flip")
+            for i in range(2):
+                for u in range(2):
+                    nc.tensor.transpose(flip[:, i, u, :], eo_turned[a][:, 2 * pair + i, u, g, :].bitcast(F32), ident[:])
+            copy(
+                out=eo_grouped[:, 2 * pair : 2 * pair + 2].rearrange("p c m t -> p (c m t)").bitcast(F32).rearrange("p (c m u) -> p c m u", c=2, u=2),
+                in_=flip[:].rearrange("p c u m -> p c m u"),
+            )
+
+        def quantise_eo(a, g):
+            nc.vector.quantize_mx(
+                out=eo_codes[:, g, a, :].bitcast(FP8X4),
+                scales=eo_scales[:, g, a, :],
+                in_=ready["eo", a, g][:].rearrange("p c m t -> p (c m t)"),
+            )
+
+        def combine(g):
+            out_rows = out[g].rearrange("(r n) m -> r n m", n=S_TILES)
+            for first in range(0, S_TILES, TILES_PER_LOAD):
+                out_sb = result.tile([P, TILES_PER_LOAD, M], F32)
+                for j in range(TILES_PER_LOAD):
+                    out_sum = banks.tile([P, M], F32, tag="bank", name="out_sum")
+                    for a in range(HALVES):
+                        cols = slice(a * P, (a + 1) * P)
+                        nc.tensor.matmul_mx(
+                            out=out_sum[:],
+                            lhsT=cw_codes[:, g, first + j, cols].bitcast(FP8X4),
+                            lhsT_scale=cw_scales[:, g, first + j, cols],
+                            rhs=eo_codes[:, g, a, :].bitcast(FP8X4),
+                            rhs_scale=eo_scales[:, g, a, :],
+                            start=(a == 0),
+                            stop=(a == HALVES - 1),
+                        )
+                    copies[j](out=out_sb[:, j, :], in_=out_sum[:])
+                nc.sync.dma_start(out=out_rows[:, first : first + TILES_PER_LOAD, :], in_=out_sb[:])
+
+        copies = (nc.scalar.copy, nc.vector.tensor_copy)
+        for e in range(E):
+            load(e)
+            group_wo(e)
+            turn_h(e)
+            turn_cw(e)
+            if e > 0:
+                expert_product(e - 1, (nc.scalar.copy, nc.scalar.copy))
+                quantise_cw(e - 1)
+            quantise_h(e)
+            quantise_wo(e)
+            if e > E_HALF:
+                turn = e - E_HALF - 1
+                turn_eo(0, turn // 2, turn % 2, nc.scalar.copy)
+                if turn % 2 == 1:
+                    quantise_eo(0, turn // 2)
+        expert_product(E - 1, copies)
+        quantise_cw(E - 1)
+        turn_eo(0, G - 1, 1, nc.scalar.copy)
+        quantise_eo(0, G - 1)
+        for g in range(G + 1):
+            if g < G:
+                for pair in range(2):
+                    turn_eo(1, g, pair, copies[pair])
+                quantise_eo(1, g)
+            if g > 0:
+                combine(g - 1)

@@ -1,4 +1,5 @@
 from contextlib import ExitStack
+from functools import partial
 
 from concourse import mybir
 from concourse.masks import make_identity
@@ -145,7 +146,7 @@ def tile_flaxpositionwisemoelayer_pb_t_kernel(tc, h, wo, combined_weights, out):
 
         def turn_eo(a, g, pair, copy):
             if pair == 0:
-                ready["eo", a, g] = grouped.tile([P, M_CHUNKS, P, PACK], BF16, align_bytes=64, name="eo_grouped")
+                ready["eo", a, g] = grouped.tile([P, M_CHUNKS, P, PACK], BF16, align_bytes=64, bufs=3, name="eo_grouped")
             eo_grouped = ready["eo", a, g]
             flip = banks.tile([P, 2, 2, P], F32, tag="bank", name="eo_flip")
             for i in range(2):
@@ -163,7 +164,8 @@ def tile_flaxpositionwisemoelayer_pb_t_kernel(tc, h, wo, combined_weights, out):
                 in_=ready["eo", a, g][:].rearrange("p c m t -> p (c m t)"),
             )
 
-        def combine(g):
+        def combine(g, later=()):
+            later = list(later)
             out_rows = out[g].rearrange("(r n) m -> r n m", n=S_TILES)
             for first in range(0, S_TILES, TILES_PER_LOAD):
                 out_sb = result.tile([P, TILES_PER_LOAD, M], F32)
@@ -182,9 +184,12 @@ def tile_flaxpositionwisemoelayer_pb_t_kernel(tc, h, wo, combined_weights, out):
                         )
                     copies[j](out=out_sb[:, j, :], in_=out_sum[:])
                 nc.sync.dma_start(out=out_rows[:, first : first + TILES_PER_LOAD, :], in_=out_sb[:])
+                if later:
+                    later[0]()
+                    later = later[1:]
 
         copies = (nc.scalar.copy, nc.vector.tensor_copy)
-        for e in range(E):
+        for e in range(E - 1):
             load(e)
             group_wo(e)
             turn_h(e)
@@ -194,19 +199,32 @@ def tile_flaxpositionwisemoelayer_pb_t_kernel(tc, h, wo, combined_weights, out):
                 quantise_cw(e - 1)
             quantise_h(e)
             quantise_wo(e)
-            if e > E_HALF:
-                turn = e - E_HALF - 1
-                turn_eo(0, turn // 2, turn % 2, nc.scalar.copy)
-                if turn % 2 == 1:
-                    quantise_eo(0, turn // 2)
-        expert_product(E - 1, copies)
-        quantise_cw(E - 1)
-        turn_eo(0, G - 1, 1, nc.scalar.copy)
-        quantise_eo(0, G - 1)
-        for g in range(G + 1):
-            if g < G:
-                for pair in range(2):
-                    turn_eo(1, g, pair, copies[pair])
-                quantise_eo(1, g)
-            if g > 0:
-                combine(g - 1)
+        last = E - 1
+        load(last)
+        group_wo(last)
+        turn_h(last)
+        expert_product(last - 1, (nc.scalar.copy, nc.scalar.copy))
+        quantise_h(last)
+        quantise_wo(last)
+        turn_eo(0, 0, 0, nc.scalar.copy)
+        turn_eo(0, 0, 1, nc.scalar.copy)
+        quantise_cw(last - 1)
+        expert_product(last, copies)
+        quantise_eo(0, 0)
+        turn_eo(0, 1, 0, copies[0])
+        turn_eo(0, 1, 1, copies[1])
+        turn_eo(1, 0, 0, copies[0])
+        turn_eo(1, 0, 1, copies[1])
+        turn_cw(last)
+        quantise_eo(1, 0)
+        quantise_eo(0, 1)
+        quantise_cw(last)
+        for g in range(G):
+            later = []
+            if g + 1 < G:
+                for a in range(HALVES):
+                    if (a, g + 1) != (0, 1):
+                        turn_eo(a, g + 1, 0, nc.scalar.copy)
+                        turn_eo(a, g + 1, 1, copies[1 - a])
+                        later.append(partial(quantise_eo, a, g + 1))
+            combine(g, later)

@@ -19,8 +19,9 @@ HALVES = K2 // K_PASS
 E_HALF = E // HALVES
 S_TILES = S // P
 M_CHUNKS = M // P
-TILES_PER_LOAD = 2
-LOADS_PER_GROUP = S_TILES // TILES_PER_LOAD
+TILES_PER_LOAD = 4
+PAIR = 2
+EARLY_TILES = E - 2
 
 FLOPS = 2 * E * G * C * H * M + 2 * G * S * K2 * M
 
@@ -30,79 +31,55 @@ def tile_flaxpositionwisemoelayer_pb_t_kernel(tc, h, wo, combined_weights, out):
     with ExitStack() as ctx:
         const = ctx.enter_context(tc.tile_pool(name="const", bufs=1))
         keep = ctx.enter_context(tc.tile_pool(name="keep", bufs=1))
-        raw = ctx.enter_context(tc.tile_pool(name="raw", bufs=5))
+        raw = ctx.enter_context(tc.tile_pool(name="raw", bufs=4))
         grouped = ctx.enter_context(tc.tile_pool(name="grouped", bufs=2))
         codes = ctx.enter_context(tc.tile_pool(name="codes", bufs=3))
-        result = ctx.enter_context(tc.tile_pool(name="result", bufs=6))
+        result = ctx.enter_context(tc.tile_pool(name="result", bufs=4))
         banks = ctx.enter_context(tc.psum_pool(name="banks", bufs=8))
         ctx.enter_context(tc.manual_schedule())
 
         ident = const.tile([P, P], F32)
         make_identity(nc, ident[:])
 
-        cw_codes = keep.tile([P, G, S_TILES, HALVES * P], U32, align_bytes=64)
-        cw_scales = keep.tile([P, G, S_TILES, HALVES * P], U8, align_bytes=64)
+        cw_codes = keep.tile([P, G * S_TILES, HALVES * P], U32, align_bytes=64)
+        cw_scales = keep.tile([P, G * S_TILES, HALVES * P], U8, align_bytes=64)
         eo_codes = keep.tile([P, G, HALVES, M], U32, align_bytes=64)
         eo_scales = keep.tile([P, G, HALVES, M], U8, align_bytes=64)
-        eo_turned = [keep.tile([P, M_CHUNKS, 2, G, E_HALF * C // 2], BF16, name="eo_turned%d" % a) for a in range(HALVES)]
+        eo_turned = [
+            keep.tile([P, M_CHUNKS, 2, G, E_HALF * C // 2], BF16, name="eo_turned%d" % a) for a in range(HALVES)
+        ]
 
+        on_scalar, on_vector = nc.scalar.copy, nc.vector.tensor_copy
         loaded = {}
         ready = {}
 
-        def load(e):
-            h_raw = raw.tile([P, 2 * H], BF16)
-            nc.sync.dma_start(out=h_raw[:], in_=h[e].rearrange("g (d n) k -> (g d) (n k)", n=2))
-            wo_raw = raw.tile([P, PACK, M], BF16)
+        def load_wo(e):
+            wo_raw = raw.tile([P, PACK, M], BF16, bufs=5)
             nc.sync.dma_start(out=wo_raw[:], in_=wo[e].rearrange("(p t) m -> p t m", t=PACK))
-            g, first = e // LOADS_PER_GROUP, (e % LOADS_PER_GROUP) * TILES_PER_LOAD
+            loaded["wo", e] = wo_raw
+
+        def load_h(e):
+            h_raw = raw.tile([P, PACK * H], BF16, bufs=3)
+            nc.sync.dma_start(out=h_raw[:], in_=h[e : e + PAIR].rearrange("e g (q j) k -> (e g q) (j k)", j=PACK))
+            loaded["h", e] = h_raw
+
+        def load_cw(first, tiles=TILES_PER_LOAD):
+            g, n = divmod(first, S_TILES)
             cw_raw = raw.tile([P, TILES_PER_LOAD, K2], BF16)
             nc.sync.dma_start(
-                out=cw_raw[:],
-                in_=combined_weights[g].rearrange("(r n) e c -> r n (e c)", n=S_TILES)[:, first : first + TILES_PER_LOAD, :],
+                out=cw_raw[:, :tiles, :],
+                in_=combined_weights[g].rearrange("(r n) e c -> r n (e c)", n=S_TILES)[:, n : n + tiles, :],
             )
-            loaded[e] = (h_raw, wo_raw, cw_raw)
-
-        def turn_h(e):
-            words = loaded[e][0][:].bitcast(F32)
-            flip = banks.tile([P, 4, P], F32, tag="bank", name="h_flip")
-            for n in range(2):
-                for k in range(2):
-                    nc.tensor.transpose(flip[:, 2 * n + k, :], words[:, n * (H // 2) + k : (n + 1) * (H // 2) : 2], ident[:])
-            h_grouped = grouped.tile([P, G * C * PACK], BF16, align_bytes=64, name="h_grouped")
-            nc.scalar.copy(
-                out=h_grouped[:].bitcast(F32).rearrange("p (u q s) -> p u q s", u=2, s=4),
-                in_=flip[:].rearrange("p s (q u) -> p u q s", u=2),
-            )
-            ready["h", e] = h_grouped
-
-        def turn_cw(e):
-            cw_grouped = grouped.tile([P, TILES_PER_LOAD, HALVES, P, PACK], BF16, align_bytes=64, name="cw_grouped")
-            for j in range(TILES_PER_LOAD):
-                words = loaded[e][2][:, j, :].bitcast(F32)
-                flip = banks.tile([P, HALVES, 2, P], F32, tag="bank", name="cw_flip")
-                for a in range(HALVES):
-                    for k in range(2):
-                        first = a * (K_PASS // 2)
-                        nc.tensor.transpose(flip[:, a, k, :], words[:, first + k : first + K_PASS // 2 : 2], ident[:])
-                nc.scalar.copy(
-                    out=cw_grouped[:, j].rearrange("p a r t -> p (a r t)").bitcast(F32).rearrange("p (a r k) -> p a r k", a=HALVES, k=2),
-                    in_=flip[:].rearrange("p a k r -> p a r k"),
-                )
-            ready["cw", e] = cw_grouped
+            for j in range(tiles):
+                loaded["cw", first + j] = cw_raw[:, j, :]
 
         def group_wo(e):
             wo_grouped = grouped.tile([P, M, PACK], BF16, align_bytes=64, name="wo_grouped")
             nc.vector.tensor_copy(
                 out=wo_grouped[:].rearrange("p (c i) t -> p c t i", i=4),
-                in_=loaded[e][1][:].rearrange("p t (c i) -> p c t i", i=4),
+                in_=loaded["wo", e][:].rearrange("p t (c i) -> p c t i", i=4),
             )
             ready["wo", e] = wo_grouped
-
-        def quantise_h(e):
-            h_codes = codes.tile([P, G * C], U32, align_bytes=64)
-            h_scales = codes.tile([P, G * C], U8, align_bytes=64)
-            nc.vector.quantize_mx(out=h_codes[:].bitcast(FP8X4), scales=h_scales[:], in_=ready["h", e][:])
-            ready["h", e] = (h_codes, h_scales)
 
         def quantise_wo(e):
             wo_codes = codes.tile([P, M], U32, align_bytes=64)
@@ -114,16 +91,34 @@ def tile_flaxpositionwisemoelayer_pb_t_kernel(tc, h, wo, combined_weights, out):
             )
             ready["wo", e] = (wo_codes, wo_scales)
 
-        def quantise_cw(e):
-            g, first = e // LOADS_PER_GROUP, (e % LOADS_PER_GROUP) * TILES_PER_LOAD
-            nc.vector.quantize_mx(
-                out=cw_codes[:, g, first : first + TILES_PER_LOAD, :].rearrange("p j w -> p (j w)").bitcast(FP8X4),
-                scales=cw_scales[:, g, first : first + TILES_PER_LOAD, :].rearrange("p j w -> p (j w)"),
-                in_=ready["cw", e][:].rearrange("p j a r t -> p (j a r t)"),
-            )
+        def turn_h(e):
+            words = loaded["h", e][:].bitcast(F32)
+            h_grouped = grouped.tile([P, PAIR, 2, G * C // PACK, 2 * PACK], BF16, align_bytes=64, name="h_grouped")
+            for u in range(2):
+                flip = banks.tile([P, 4, P], F32, tag="bank", name="h_flip")
+                for n in range(2):
+                    for k in range(2):
+                        first = (2 * u + n) * (H // 2)
+                        nc.tensor.transpose(flip[:, 2 * n + k, :], words[:, first + k : first + H // 2 : 2], ident[:])
+                nc.scalar.copy(
+                    out=h_grouped[:, :, u].rearrange("p e q s -> p e (q s)").bitcast(F32).rearrange("p e (q s) -> p e q s", s=4),
+                    in_=flip[:].rearrange("p s (e q) -> p e q s", e=PAIR),
+                )
+            ready["h", e] = h_grouped
 
-        def expert_product(e, engines):
-            a, e_in = e // E_HALF, e % E_HALF
+        def quantise_h(e):
+            h_codes = codes.tile([P, PAIR, G * C], U32, align_bytes=64)
+            h_scales = codes.tile([P, PAIR, G * C], U8, align_bytes=64)
+            nc.vector.quantize_mx(
+                out=h_codes[:].rearrange("p e w -> p (e w)").bitcast(FP8X4),
+                scales=h_scales[:].rearrange("p e w -> p (e w)"),
+                in_=ready["h", e][:].rearrange("p e u q s -> p (e u q s)"),
+            )
+            for i in range(PAIR):
+                ready["h", e + i] = (h_codes[:, i, :], h_scales[:, i, :])
+
+        def expert_product(e, copies):
+            a, e_in = divmod(e, E_HALF)
             h_codes, h_scales = ready["h", e]
             wo_codes, wo_scales = ready["wo", e]
             for pair in range(M_CHUNKS // 2):
@@ -134,28 +129,65 @@ def tile_flaxpositionwisemoelayer_pb_t_kernel(tc, h, wo, combined_weights, out):
                         out=eo_sum[:, i, :],
                         lhsT=wo_codes[:, cols].bitcast(FP8X4),
                         lhsT_scale=wo_scales[:, cols],
-                        rhs=h_codes[:].bitcast(FP8X4),
-                        rhs_scale=h_scales[:],
+                        rhs=h_codes.bitcast(FP8X4),
+                        rhs_scale=h_scales,
                         start=True,
                         stop=True,
                     )
-                engines[pair](
-                    out=eo_turned[a][:, 2 * pair : 2 * pair + 2, :, :, e_in * C // 2 : (e_in + 1) * C // 2].rearrange("p c u g w -> p (c u g) w"),
+                slots = slice(e_in * C // 2, (e_in + 1) * C // 2)
+                copies[pair](
+                    out=eo_turned[a][:, 2 * pair : 2 * pair + 2, :, :, slots].rearrange("p c u g w -> p (c u g) w"),
                     in_=eo_sum[:].rearrange("p c (x w) -> p (c x) w", w=C // 2),
                 )
 
-        def turn_eo(a, g, pair, copy):
-            if pair == 0:
-                ready["eo", a, g] = grouped.tile([P, M_CHUNKS, P, PACK], BF16, align_bytes=64, bufs=3, name="eo_grouped")
-            eo_grouped = ready["eo", a, g]
-            flip = banks.tile([P, 2, 2, P], F32, tag="bank", name="eo_flip")
-            for i in range(2):
-                for u in range(2):
-                    nc.tensor.transpose(flip[:, i, u, :], eo_turned[a][:, 2 * pair + i, u, g, :].bitcast(F32), ident[:])
-            copy(
-                out=eo_grouped[:, 2 * pair : 2 * pair + 2].rearrange("p c m t -> p (c m t)").bitcast(F32).rearrange("p (c m u) -> p c m u", c=2, u=2),
-                in_=flip[:].rearrange("p c u m -> p c m u"),
+        def sort_cw(first, copy):
+            cw_sorted = grouped.tile([P, PAIR, HALVES, 2, P], F32, name="cw_sorted")
+            for j in range(PAIR):
+                copy(
+                    out=cw_sorted[:, j],
+                    in_=loaded["cw", first + j].bitcast(F32).rearrange("p (a w k) -> p a k w", a=HALVES, k=2),
+                )
+            ready["sorted", first] = cw_sorted
+
+        def turn_cw(first, copies):
+            cw_grouped = grouped.tile([P, PAIR, HALVES, P, PACK], BF16, align_bytes=64, name="cw_grouped")
+            for j in range(PAIR):
+                flip = banks.tile([P, HALVES, 2, P], F32, tag="bank", name="cw_flip")
+                for a in range(HALVES):
+                    for k in range(2):
+                        if ("sorted", first) in ready:
+                            words = ready["sorted", first][:, j, a, k, :]
+                        else:
+                            words = loaded["cw", first + j].bitcast(F32)[
+                                :, a * K_PASS // 2 + k : (a + 1) * K_PASS // 2 : 2
+                            ]
+                        nc.tensor.transpose(flip[:, a, k, :], words, ident[:])
+                copies[j](
+                    out=cw_grouped[:, j].rearrange("p a r t -> p (a r t)").bitcast(F32).rearrange("p (a r k) -> p a r k", a=HALVES, k=2),
+                    in_=flip[:].rearrange("p a k r -> p a r k"),
+                )
+            ready["cw", first] = cw_grouped
+
+        def quantise_cw(first):
+            tiles = slice(first, first + PAIR)
+            nc.vector.quantize_mx(
+                out=cw_codes[:, tiles, :].rearrange("p j w -> p (j w)").bitcast(FP8X4),
+                scales=cw_scales[:, tiles, :].rearrange("p j w -> p (j w)"),
+                in_=ready["cw", first][:].rearrange("p j a r t -> p (j a r t)"),
             )
+
+        def turn_eo(a, g, copies):
+            eo_grouped = grouped.tile([P, M_CHUNKS, P, PACK], BF16, align_bytes=64, bufs=3, name="eo_grouped")
+            for pair in range(M_CHUNKS // 2):
+                flip = banks.tile([P, 2, 2, P], F32, tag="bank", name="eo_flip")
+                for i in range(2):
+                    for u in range(2):
+                        nc.tensor.transpose(flip[:, i, u, :], eo_turned[a][:, 2 * pair + i, u, g, :].bitcast(F32), ident[:])
+                copies[pair](
+                    out=eo_grouped[:, 2 * pair : 2 * pair + 2].rearrange("p c m t -> p (c m t)").bitcast(F32).rearrange("p (c m u) -> p c m u", c=2, u=2),
+                    in_=flip[:].rearrange("p c u m -> p c m u"),
+                )
+            ready["eo", a, g] = eo_grouped
 
         def quantise_eo(a, g):
             nc.vector.quantize_mx(
@@ -164,67 +196,98 @@ def tile_flaxpositionwisemoelayer_pb_t_kernel(tc, h, wo, combined_weights, out):
                 in_=ready["eo", a, g][:].rearrange("p c m t -> p (c m t)"),
             )
 
-        def combine(g, later=()):
-            later = list(later)
+        def combine(g, first):
             out_rows = out[g].rearrange("(r n) m -> r n m", n=S_TILES)
-            for first in range(0, S_TILES, TILES_PER_LOAD):
-                out_sb = result.tile([P, TILES_PER_LOAD, M], F32)
-                for j in range(TILES_PER_LOAD):
-                    out_sum = banks.tile([P, M], F32, tag="bank", name="out_sum")
-                    for a in range(HALVES):
-                        cols = slice(a * P, (a + 1) * P)
-                        nc.tensor.matmul_mx(
-                            out=out_sum[:],
-                            lhsT=cw_codes[:, g, first + j, cols].bitcast(FP8X4),
-                            lhsT_scale=cw_scales[:, g, first + j, cols],
-                            rhs=eo_codes[:, g, a, :].bitcast(FP8X4),
-                            rhs_scale=eo_scales[:, g, a, :],
-                            start=(a == 0),
-                            stop=(a == HALVES - 1),
-                        )
-                    copies[j](out=out_sb[:, j, :], in_=out_sum[:])
-                nc.sync.dma_start(out=out_rows[:, first : first + TILES_PER_LOAD, :], in_=out_sb[:])
-                if later:
-                    later[0]()
-                    later = later[1:]
-
-        copies = (nc.scalar.copy, nc.vector.tensor_copy)
-        for e in range(E - 1):
-            load(e)
-            group_wo(e)
-            turn_h(e)
-            turn_cw(e)
-            if e > 0:
-                expert_product(e - 1, (nc.scalar.copy, nc.scalar.copy))
-                quantise_cw(e - 1)
-            quantise_h(e)
-            quantise_wo(e)
-        last = E - 1
-        load(last)
-        group_wo(last)
-        turn_h(last)
-        expert_product(last - 1, (nc.scalar.copy, nc.scalar.copy))
-        quantise_h(last)
-        quantise_wo(last)
-        turn_eo(0, 0, 0, nc.scalar.copy)
-        turn_eo(0, 0, 1, nc.scalar.copy)
-        quantise_cw(last - 1)
-        expert_product(last, copies)
-        quantise_eo(0, 0)
-        turn_eo(0, 1, 0, copies[0])
-        turn_eo(0, 1, 1, copies[1])
-        turn_eo(1, 0, 0, copies[0])
-        turn_eo(1, 0, 1, copies[1])
-        turn_cw(last)
-        quantise_eo(1, 0)
-        quantise_eo(0, 1)
-        quantise_cw(last)
-        for g in range(G):
-            later = []
-            if g + 1 < G:
+            apart = g == G - 1 and first == S_TILES - PAIR
+            out_sb = result.tile([P, PAIR, M], F32)
+            for j in range(PAIR):
+                out_sum = banks.tile([P, M], F32, tag="bank", name="out_sum")
                 for a in range(HALVES):
-                    if (a, g + 1) != (0, 1):
-                        turn_eo(a, g + 1, 0, nc.scalar.copy)
-                        turn_eo(a, g + 1, 1, copies[1 - a])
-                        later.append(partial(quantise_eo, a, g + 1))
-            combine(g, later)
+                    cols = slice(a * P, (a + 1) * P)
+                    tile = g * S_TILES + first + j
+                    nc.tensor.matmul_mx(
+                        out=out_sum[:],
+                        lhsT=cw_codes[:, tile, cols].bitcast(FP8X4),
+                        lhsT_scale=cw_scales[:, tile, cols],
+                        rhs=eo_codes[:, g, a, :].bitcast(FP8X4),
+                        rhs_scale=eo_scales[:, g, a, :],
+                        start=(a == 0),
+                        stop=(a == HALVES - 1),
+                    )
+                (on_scalar, on_vector)[j](out=out_sb[:, j, :], in_=out_sum[:])
+                if apart:
+                    nc.sync.dma_start(out=out_rows[:, first + j, :], in_=out_sb[:, j, :])
+            if not apart:
+                nc.sync.dma_start(out=out_rows[:, first : first + PAIR, :], in_=out_sb[:])
+
+        SCALAR_ONLY = (on_scalar, on_scalar)
+        BOTH = (on_scalar, on_vector)
+        load_wo(0)
+        load_h(0)
+        load_wo(1)
+        load_h(2)
+        load_wo(2)
+        load_cw(0, PAIR)
+        turn_h(0)
+        turned = [partial(quantise_h, 0)]
+        for e in range(E):
+            if e + 3 < E:
+                load_wo(e + 3)
+            if e % 2 == 0 and e + 4 < E:
+                load_h(e + 4)
+            if e == 1:
+                load_cw(PAIR, PAIR)
+            elif e % 4 == 3 and e + 1 < EARLY_TILES:
+                load_cw(e + 1)
+            group_wo(e)
+            if e > 0:
+                for quantise in turned:
+                    quantise()
+                turned = []
+            if e == E - 1:
+                turn_eo(0, 0, SCALAR_ONLY)
+            elif e % 2 == 1:
+                turn_h(e + 1)
+                turned = [partial(quantise_h, e + 1)]
+            elif e > 0:
+                turn_cw(e - 2, SCALAR_ONLY)
+                turned = [partial(quantise_cw, e - 2)]
+            if e > 0:
+                expert_product(e - 1, SCALAR_ONLY)
+            quantise_wo(e)
+        for first in range(E, G * S_TILES, TILES_PER_LOAD):
+            load_cw(first)
+
+        turn_eo(0, 1, (on_vector, on_vector))
+        expert_product(E - 1, BOTH)
+        turn_eo(1, 0, BOTH)
+        quantise_eo(0, 0)
+        turn_eo(1, 1, SCALAR_ONLY)
+        turn_cw(EARLY_TILES, SCALAR_ONLY)
+        quantise_eo(1, 0)
+
+        late = list(range(EARLY_TILES + PAIR, G * S_TILES, PAIR))
+        turns = [(0, 2), (1, 2), (0, 3), (1, 3)]
+        jobs = [late[:2]] + [[turns[i], late[i + 2]] for i in range(len(turns))] + [late[len(turns) + 2:]]
+        sort_cw(late[0], on_vector)
+        sort_cw(late[1], on_vector)
+        waiting = [partial(quantise_eo, 0, 1), partial(quantise_eo, 1, 1), partial(quantise_cw, EARLY_TILES)]
+        for i in range(2 * G):
+            g, half = divmod(i, 2)
+            combine(g, 4 * half)
+            for quantise in waiting:
+                quantise()
+            waiting = []
+            if i < len(jobs):
+                for job in jobs[i]:
+                    if isinstance(job, int):
+                        turn_cw(job, SCALAR_ONLY)
+                        waiting.append(partial(quantise_cw, job))
+                    else:
+                        turn_eo(job[0], job[1], BOTH)
+                        waiting.append(partial(quantise_eo, job[0], job[1]))
+            combine(g, 4 * half + PAIR)
+            if i + 1 < len(jobs):
+                for job in jobs[i + 1]:
+                    if isinstance(job, int):
+                        sort_cw(job, on_vector)

@@ -33,7 +33,7 @@ def tile_flaxpositionwisemoelayer_pb_t_kernel(tc, h, wo, combined_weights, out):
         keep = ctx.enter_context(tc.tile_pool(name="keep", bufs=1))
         raw = ctx.enter_context(tc.tile_pool(name="raw", bufs=4))
         grouped = ctx.enter_context(tc.tile_pool(name="grouped", bufs=2))
-        codes = ctx.enter_context(tc.tile_pool(name="codes", bufs=3))
+        codes = ctx.enter_context(tc.tile_pool(name="codes", bufs=2))
         result = ctx.enter_context(tc.tile_pool(name="result", bufs=4))
         banks = ctx.enter_context(tc.psum_pool(name="banks", bufs=8))
         ctx.enter_context(tc.manual_schedule())
@@ -54,7 +54,7 @@ def tile_flaxpositionwisemoelayer_pb_t_kernel(tc, h, wo, combined_weights, out):
         ready = {}
 
         def load_wo(e):
-            wo_raw = raw.tile([P, PACK, M], BF16, bufs=5)
+            wo_raw = raw.tile([P, PACK, M], BF16, bufs=4)
             nc.sync.dma_start(out=wo_raw[:], in_=wo[e].rearrange("(p t) m -> p t m", t=PACK))
             loaded["wo", e] = wo_raw
 
@@ -72,6 +72,8 @@ def tile_flaxpositionwisemoelayer_pb_t_kernel(tc, h, wo, combined_weights, out):
             )
             for j in range(tiles):
                 loaded["cw", first + j] = cw_raw[:, j, :]
+                if j % PAIR == 0:
+                    loaded["pair", first + j] = cw_raw[:, j : j + PAIR, :]
 
         def group_wo(e):
             wo_grouped = grouped.tile([P, M, PACK], BF16, align_bytes=64, name="wo_grouped")
@@ -141,16 +143,15 @@ def tile_flaxpositionwisemoelayer_pb_t_kernel(tc, h, wo, combined_weights, out):
                 )
 
         def sort_cw(first, copy):
-            cw_sorted = grouped.tile([P, PAIR, HALVES, 2, P], F32, name="cw_sorted")
-            for j in range(PAIR):
-                copy(
-                    out=cw_sorted[:, j],
-                    in_=loaded["cw", first + j].bitcast(F32).rearrange("p (a w k) -> p a k w", a=HALVES, k=2),
-                )
+            cw_sorted = grouped.tile([P, PAIR, HALVES, 2, P], F32, bufs=3, name="cw_sorted")
+            copy(
+                out=cw_sorted[:].rearrange("p j a k w -> p (j a) k w"),
+                in_=loaded["pair", first].rearrange("p j x -> p (j x)").bitcast(F32).rearrange("p (b w k) -> p b k w", b=PAIR * HALVES, k=2),
+            )
             ready["sorted", first] = cw_sorted
 
         def turn_cw(first, copies):
-            cw_grouped = grouped.tile([P, PAIR, HALVES, P, PACK], BF16, align_bytes=64, name="cw_grouped")
+            cw_grouped = grouped.tile([P, PAIR, HALVES, P, PACK], BF16, align_bytes=64, bufs=4, name="cw_grouped")
             for j in range(PAIR):
                 flip = banks.tile([P, HALVES, 2, P], F32, tag="bank", name="cw_flip")
                 for a in range(HALVES):
@@ -214,7 +215,11 @@ def tile_flaxpositionwisemoelayer_pb_t_kernel(tc, h, wo, combined_weights, out):
                         start=(a == 0),
                         stop=(a == HALVES - 1),
                     )
-                (on_scalar, on_vector)[j](out=out_sb[:, j, :], in_=out_sum[:])
+                if apart and j == PAIR - 1:
+                    for copy, cols in ((on_scalar, slice(0, M // 2)), (on_vector, slice(M // 2, M))):
+                        copy(out=out_sb[:, j, cols], in_=out_sum[:, cols])
+                else:
+                    (on_scalar, on_vector)[j](out=out_sb[:, j, :], in_=out_sum[:])
                 if apart:
                     nc.sync.dma_start(out=out_rows[:, first + j, :], in_=out_sb[:, j, :])
             if not apart:
@@ -251,7 +256,8 @@ def tile_flaxpositionwisemoelayer_pb_t_kernel(tc, h, wo, combined_weights, out):
                 turned = [partial(quantise_h, e + 1)]
             elif e > 0:
                 turn_cw(e - 2, SCALAR_ONLY)
-                turned = [partial(quantise_cw, e - 2)]
+                if e - 2 < EARLY_TILES - 4:
+                    turned = [partial(quantise_cw, e - 2)]
             if e > 0:
                 expert_product(e - 1, SCALAR_ONLY)
             quantise_wo(e)
@@ -260,6 +266,7 @@ def tile_flaxpositionwisemoelayer_pb_t_kernel(tc, h, wo, combined_weights, out):
 
         turn_eo(0, 1, (on_vector, on_vector))
         expert_product(E - 1, BOTH)
+        quantise_cw(EARLY_TILES - 4)
         turn_eo(1, 0, BOTH)
         quantise_eo(0, 0)
         turn_eo(1, 1, SCALAR_ONLY)
@@ -268,26 +275,28 @@ def tile_flaxpositionwisemoelayer_pb_t_kernel(tc, h, wo, combined_weights, out):
 
         late = list(range(EARLY_TILES + PAIR, G * S_TILES, PAIR))
         turns = [(0, 2), (1, 2), (0, 3), (1, 3)]
-        jobs = [late[:2]] + [[turns[i], late[i + 2]] for i in range(len(turns))] + [late[len(turns) + 2:]]
-        sort_cw(late[0], on_vector)
-        sort_cw(late[1], on_vector)
-        waiting = [partial(quantise_eo, 0, 1), partial(quantise_eo, 1, 1), partial(quantise_cw, EARLY_TILES)]
-        for i in range(2 * G):
-            g, half = divmod(i, 2)
-            combine(g, 4 * half)
+        jobs = {1: late[:2], 10: late[6:7], 12: late[7:]}
+        for i in range(len(turns)):
+            jobs[2 * i + 3] = [turns[i], late[i + 2]]
+        waiting = [partial(quantise_cw, first) for first in range(EARLY_TILES - 4, EARLY_TILES, PAIR)][1:]
+        waiting += [partial(quantise_eo, 0, 1), partial(quantise_eo, 1, 1), partial(quantise_cw, EARLY_TILES)]
+        for i in [1,2]:
+            for job in jobs.get(i, []):
+                if isinstance(job, int):
+                    sort_cw(job, on_vector)
+        for i in range(G * S_TILES // PAIR):
+            turned = []
+            for job in jobs.get(i, []):
+                if isinstance(job, int):
+                    turn_cw(job, SCALAR_ONLY)
+                    turned.append(partial(quantise_cw, job))
+                else:
+                    turn_eo(job[0], job[1], SCALAR_ONLY)
+                    turned.append(partial(quantise_eo, job[0], job[1]))
+            combine(i * PAIR // S_TILES, i * PAIR % S_TILES)
             for quantise in waiting:
                 quantise()
-            waiting = []
-            if i < len(jobs):
-                for job in jobs[i]:
-                    if isinstance(job, int):
-                        turn_cw(job, SCALAR_ONLY)
-                        waiting.append(partial(quantise_cw, job))
-                    else:
-                        turn_eo(job[0], job[1], BOTH)
-                        waiting.append(partial(quantise_eo, job[0], job[1]))
-            combine(g, 4 * half + PAIR)
-            if i + 1 < len(jobs):
-                for job in jobs[i + 1]:
-                    if isinstance(job, int):
-                        sort_cw(job, on_vector)
+            waiting = turned
+            for job in jobs.get(i + 3, []):
+                if isinstance(job, int):
+                    sort_cw(job, on_vector)

@@ -59,7 +59,7 @@ def tile_flaxpositionwisemoelayer_pb_t_kernel(tc, h, wo, combined_weights, out):
             loaded["wo", e] = wo_raw
 
         def load_h(e):
-            h_raw = raw.tile([P, PACK * H], BF16, bufs=3)
+            h_raw = raw.tile([P, PACK * H], BF16, bufs=2)
             nc.sync.dma_start(out=h_raw[:], in_=h[e : e + PAIR].rearrange("e g (q j) k -> (e g q) (j k)", j=PACK))
             loaded["h", e] = h_raw
 
@@ -150,9 +150,11 @@ def tile_flaxpositionwisemoelayer_pb_t_kernel(tc, h, wo, combined_weights, out):
             )
             ready["sorted", first] = cw_sorted
 
-        def turn_cw(first, copies):
-            cw_grouped = grouped.tile([P, PAIR, HALVES, P, PACK], BF16, align_bytes=64, bufs=4, name="cw_grouped")
-            for j in range(PAIR):
+        def turn_cw(first, copies, tiles=range(PAIR)):
+            if 0 in tiles:
+                ready["cw", first] = grouped.tile([P, PAIR, HALVES, P, PACK], BF16, align_bytes=64, bufs=4, name="cw_grouped")
+            cw_grouped = ready["cw", first]
+            for j in tiles:
                 flip = banks.tile([P, HALVES, 2, P], F32, tag="bank", name="cw_flip")
                 for a in range(HALVES):
                     for k in range(2):
@@ -167,7 +169,6 @@ def tile_flaxpositionwisemoelayer_pb_t_kernel(tc, h, wo, combined_weights, out):
                     out=cw_grouped[:, j].rearrange("p a r t -> p (a r t)").bitcast(F32).rearrange("p (a r k) -> p a r k", a=HALVES, k=2),
                     in_=flip[:].rearrange("p a k r -> p a r k"),
                 )
-            ready["cw", first] = cw_grouped
 
         def quantise_cw(first):
             tiles = slice(first, first + PAIR)
@@ -178,7 +179,7 @@ def tile_flaxpositionwisemoelayer_pb_t_kernel(tc, h, wo, combined_weights, out):
             )
 
         def turn_eo(a, g, copies):
-            eo_grouped = grouped.tile([P, M_CHUNKS, P, PACK], BF16, align_bytes=64, bufs=3, name="eo_grouped")
+            eo_grouped = grouped.tile([P, M_CHUNKS, P, PACK], BF16, align_bytes=64, bufs=4, name="eo_grouped")
             for pair in range(M_CHUNKS // 2):
                 flip = banks.tile([P, 2, 2, P], F32, tag="bank", name="eo_flip")
                 for i in range(2):
@@ -202,24 +203,23 @@ def tile_flaxpositionwisemoelayer_pb_t_kernel(tc, h, wo, combined_weights, out):
             apart = g == G - 1 and first == S_TILES - PAIR
             out_sb = result.tile([P, PAIR, M], F32)
             for j in range(PAIR):
-                out_sum = banks.tile([P, M], F32, tag="bank", name="out_sum")
-                for a in range(HALVES):
-                    cols = slice(a * P, (a + 1) * P)
-                    tile = g * S_TILES + first + j
-                    nc.tensor.matmul_mx(
-                        out=out_sum[:],
-                        lhsT=cw_codes[:, tile, cols].bitcast(FP8X4),
-                        lhsT_scale=cw_scales[:, tile, cols],
-                        rhs=eo_codes[:, g, a, :].bitcast(FP8X4),
-                        rhs_scale=eo_scales[:, g, a, :],
-                        start=(a == 0),
-                        stop=(a == HALVES - 1),
-                    )
-                if apart and j == PAIR - 1:
-                    for copy, cols in ((on_scalar, slice(0, M // 2)), (on_vector, slice(M // 2, M))):
-                        copy(out=out_sb[:, j, cols], in_=out_sum[:, cols])
-                else:
-                    (on_scalar, on_vector)[j](out=out_sb[:, j, :], in_=out_sum[:])
+                parts = 2 if apart and j == PAIR - 1 else 1
+                for part in range(parts):
+                    channels = slice(part * M // parts, (part + 1) * M // parts)
+                    out_sum = banks.tile([P, M // parts], F32, tag="bank", name="out_sum")
+                    for a in range(HALVES):
+                        cols = slice(a * P, (a + 1) * P)
+                        tile = g * S_TILES + first + j
+                        nc.tensor.matmul_mx(
+                            out=out_sum[:],
+                            lhsT=cw_codes[:, tile, cols].bitcast(FP8X4),
+                            lhsT_scale=cw_scales[:, tile, cols],
+                            rhs=eo_codes[:, g, a, channels].bitcast(FP8X4),
+                            rhs_scale=eo_scales[:, g, a, channels],
+                            start=(a == 0),
+                            stop=(a == HALVES - 1),
+                        )
+                    (on_scalar, on_vector)[(j + part) % 2](out=out_sb[:, j, channels], in_=out_sum[:])
                 if apart:
                     nc.sync.dma_start(out=out_rows[:, first + j, :], in_=out_sb[:, j, :])
             if not apart:
@@ -242,8 +242,8 @@ def tile_flaxpositionwisemoelayer_pb_t_kernel(tc, h, wo, combined_weights, out):
                 load_h(e + 4)
             if e == 1:
                 load_cw(PAIR, PAIR)
-            elif e % 4 == 3 and e + 1 < EARLY_TILES:
-                load_cw(e + 1)
+            elif e % 2 == 1 and e + 1 < EARLY_TILES:
+                load_cw(e + 1, PAIR)
             group_wo(e)
             if e > 0:
                 for quantise in turned:
@@ -261,24 +261,25 @@ def tile_flaxpositionwisemoelayer_pb_t_kernel(tc, h, wo, combined_weights, out):
             if e > 0:
                 expert_product(e - 1, SCALAR_ONLY)
             quantise_wo(e)
+        load_cw(EARLY_TILES, PAIR)
         for first in range(E, G * S_TILES, TILES_PER_LOAD):
             load_cw(first)
 
         turn_eo(0, 1, (on_vector, on_vector))
         expert_product(E - 1, BOTH)
-        quantise_cw(EARLY_TILES - 4)
-        turn_eo(1, 0, BOTH)
+        turn_cw(EARLY_TILES, SCALAR_ONLY, range(1))
         quantise_eo(0, 0)
+        turn_eo(1, 0, BOTH)
         turn_eo(1, 1, SCALAR_ONLY)
-        turn_cw(EARLY_TILES, SCALAR_ONLY)
         quantise_eo(1, 0)
+        turn_cw(EARLY_TILES, SCALAR_ONLY, range(1, PAIR))
 
         late = list(range(EARLY_TILES + PAIR, G * S_TILES, PAIR))
         turns = [(0, 2), (1, 2), (0, 3), (1, 3)]
         jobs = {1: late[:2], 10: late[6:7], 12: late[7:]}
         for i in range(len(turns)):
             jobs[2 * i + 3] = [turns[i], late[i + 2]]
-        waiting = [partial(quantise_cw, first) for first in range(EARLY_TILES - 4, EARLY_TILES, PAIR)][1:]
+        waiting = [partial(quantise_cw, first) for first in range(EARLY_TILES - 4, EARLY_TILES, PAIR)]
         waiting += [partial(quantise_eo, 0, 1), partial(quantise_eo, 1, 1), partial(quantise_cw, EARLY_TILES)]
         for i in [1,2]:
             for job in jobs.get(i, []):

@@ -19,7 +19,6 @@ HALVES = K2 // K_PASS
 E_HALF = E // HALVES
 S_TILES = S // P
 M_CHUNKS = M // P
-TILES_PER_LOAD = 4
 PAIR = 2
 EARLY_TILES = E - 2
 
@@ -54,7 +53,7 @@ def tile_flaxpositionwisemoelayer_pb_t_kernel(tc, h, wo, combined_weights, out):
         ready = {}
 
         def load_wo(e):
-            wo_raw = raw.tile([P, PACK, M], BF16, bufs=4)
+            wo_raw = raw.tile([P, PACK, M], BF16, bufs=5)
             nc.sync.dma_start(out=wo_raw[:], in_=wo[e].rearrange("(p t) m -> p t m", t=PACK))
             loaded["wo", e] = wo_raw
 
@@ -63,17 +62,14 @@ def tile_flaxpositionwisemoelayer_pb_t_kernel(tc, h, wo, combined_weights, out):
             nc.sync.dma_start(out=h_raw[:], in_=h[e : e + PAIR].rearrange("e g (q j) k -> (e g q) (j k)", j=PACK))
             loaded["h", e] = h_raw
 
-        def load_cw(first, tiles=TILES_PER_LOAD):
+        def load_cw(first):
             g, n = divmod(first, S_TILES)
-            cw_raw = raw.tile([P, TILES_PER_LOAD, K2], BF16)
+            cw_raw = raw.tile([P, PAIR, K2], BF16, bufs=6)
             nc.sync.dma_start(
-                out=cw_raw[:, :tiles, :],
-                in_=combined_weights[g].rearrange("(r n) e c -> r n (e c)", n=S_TILES)[:, n : n + tiles, :],
+                out=cw_raw[:],
+                in_=combined_weights[g].rearrange("(r n) e c -> r n (e c)", n=S_TILES)[:, n : n + PAIR, :],
             )
-            for j in range(tiles):
-                loaded["cw", first + j] = cw_raw[:, j, :]
-                if j % PAIR == 0:
-                    loaded["pair", first + j] = cw_raw[:, j : j + PAIR, :]
+            loaded["cw", first] = cw_raw
 
         def group_wo(e):
             wo_grouped = grouped.tile([P, M, PACK], BF16, align_bytes=64, name="wo_grouped")
@@ -146,7 +142,7 @@ def tile_flaxpositionwisemoelayer_pb_t_kernel(tc, h, wo, combined_weights, out):
             cw_sorted = grouped.tile([P, PAIR, HALVES, 2, P], F32, bufs=3, name="cw_sorted")
             copy(
                 out=cw_sorted[:].rearrange("p j a k w -> p (j a) k w"),
-                in_=loaded["pair", first].rearrange("p j x -> p (j x)").bitcast(F32).rearrange("p (b w k) -> p b k w", b=PAIR * HALVES, k=2),
+                in_=loaded["cw", first][:].rearrange("p j x -> p (j x)").bitcast(F32).rearrange("p (b w k) -> p b k w", b=PAIR * HALVES, k=2),
             )
             ready["sorted", first] = cw_sorted
 
@@ -161,7 +157,7 @@ def tile_flaxpositionwisemoelayer_pb_t_kernel(tc, h, wo, combined_weights, out):
                         if ("sorted", first) in ready:
                             words = ready["sorted", first][:, j, a, k, :]
                         else:
-                            words = loaded["cw", first + j].bitcast(F32)[
+                            words = loaded["cw", first][:, j, :].bitcast(F32)[
                                 :, a * K_PASS // 2 + k : (a + 1) * K_PASS // 2 : 2
                             ]
                         nc.tensor.transpose(flip[:, a, k, :], words, ident[:])
@@ -232,7 +228,7 @@ def tile_flaxpositionwisemoelayer_pb_t_kernel(tc, h, wo, combined_weights, out):
         load_wo(1)
         load_h(2)
         load_wo(2)
-        load_cw(0, PAIR)
+        load_cw(0)
         turn_h(0)
         turned = [partial(quantise_h, 0)]
         for e in range(E):
@@ -241,9 +237,9 @@ def tile_flaxpositionwisemoelayer_pb_t_kernel(tc, h, wo, combined_weights, out):
             if e % 2 == 0 and e + 4 < E:
                 load_h(e + 4)
             if e == 1:
-                load_cw(PAIR, PAIR)
+                load_cw(PAIR)
             elif e % 2 == 1 and e + 1 < EARLY_TILES:
-                load_cw(e + 1, PAIR)
+                load_cw(e + 1)
             group_wo(e)
             if e > 0:
                 for quantise in turned:
@@ -261,8 +257,7 @@ def tile_flaxpositionwisemoelayer_pb_t_kernel(tc, h, wo, combined_weights, out):
             if e > 0:
                 expert_product(e - 1, SCALAR_ONLY)
             quantise_wo(e)
-        load_cw(EARLY_TILES, PAIR)
-        for first in range(E, G * S_TILES, TILES_PER_LOAD):
+        for first in range(EARLY_TILES, G * S_TILES, PAIR):
             load_cw(first)
 
         turn_eo(0, 1, (on_vector, on_vector))
@@ -276,9 +271,7 @@ def tile_flaxpositionwisemoelayer_pb_t_kernel(tc, h, wo, combined_weights, out):
 
         late = list(range(EARLY_TILES + PAIR, G * S_TILES, PAIR))
         turns = [(0, 2), (1, 2), (0, 3), (1, 3)]
-        jobs = {1: late[:2], 10: late[6:7], 12: late[7:]}
-        for i in range(len(turns)):
-            jobs[2 * i + 3] = [turns[i], late[i + 2]]
+        jobs = {1: [late[0], turns[0], late[1]], 4: [turns[1], late[2]], 6: [turns[2], late[3]], 8: [turns[3], late[4]], 10: [late[5], late[6]], 12: late[7:]}
         waiting = [partial(quantise_cw, first) for first in range(EARLY_TILES - 4, EARLY_TILES, PAIR)]
         waiting += [partial(quantise_eo, 0, 1), partial(quantise_eo, 1, 1), partial(quantise_cw, EARLY_TILES)]
         for i in [1,2]:

@@ -141,8 +141,8 @@ def tile_flaxpositionwisemoelayer_pb_t_kernel(tc, h, wo, combined_weights, out):
         def sort_cw(first, copy):
             cw_sorted = grouped.tile([P, PAIR, HALVES, 2, P], F32, bufs=3, name="cw_sorted")
             copy(
-                out=cw_sorted[:].rearrange("p j a k w -> p (j a) k w"),
-                in_=loaded["cw", first][:].rearrange("p j x -> p (j x)").bitcast(F32).rearrange("p (b w k) -> p b k w", b=PAIR * HALVES, k=2),
+                out=cw_sorted[:].rearrange("p j a k w -> p (j a) w k"),
+                in_=loaded["cw", first][:].rearrange("p j x -> p (j x)").bitcast(F32).rearrange("p (b w k) -> p b w k", b=PAIR * HALVES, k=2),
             )
             ready["sorted", first] = cw_sorted
 

from contextlib import ExitStack
from functools import partial

from concourse import mybir
from concourse.masks import make_identity

BF16 = mybir.dt.bfloat16
F32 = mybir.dt.float32
U32 = mybir.dt.uint32
U8 = mybir.dt.uint8
FP8X4 = mybir.dt.float8_e4m3fn_x4

E, G, C, H, M, S = 16, 4, 64, 512, 512, 1024
P = 128
PACK = 4
K_PASS = P * PACK
K2 = E * C
HALVES = K2 // K_PASS
E_HALF = E // HALVES
S_TILES = S // P
M_CHUNKS = M // P
PAIR = 2
EARLY_TILES = E - 2

FLOPS = 2 * E * G * C * H * M + 2 * G * S * K2 * M


def tile_flaxpositionwisemoelayer_pb_t_kernel(tc, h, wo, combined_weights, out):
    nc = tc.nc
    with ExitStack() as ctx:
        const = ctx.enter_context(tc.tile_pool(name="const", bufs=1))
        keep = ctx.enter_context(tc.tile_pool(name="keep", bufs=1))
        raw = ctx.enter_context(tc.tile_pool(name="raw", bufs=4))
        grouped = ctx.enter_context(tc.tile_pool(name="grouped", bufs=2))
        codes = ctx.enter_context(tc.tile_pool(name="codes", bufs=2))
        result = ctx.enter_context(tc.tile_pool(name="result", bufs=4))
        banks = ctx.enter_context(tc.psum_pool(name="banks", bufs=8))
        ctx.enter_context(tc.manual_schedule())

        ident = const.tile([P, P], F32)
        make_identity(nc, ident[:])

        cw_codes = keep.tile([P, G * S_TILES, HALVES * P], U32, align_bytes=64)
        cw_scales = keep.tile([P, G * S_TILES, HALVES * P], U8, align_bytes=64)
        eo_codes = keep.tile([P, G, HALVES, M], U32, align_bytes=64)
        eo_scales = keep.tile([P, G, HALVES, M], U8, align_bytes=64)
        eo_turned = [
            keep.tile([P, M_CHUNKS, 2, G, E_HALF * C // 2], BF16, name="eo_turned%d" % a) for a in range(HALVES)
        ]

        on_scalar, on_vector = nc.scalar.copy, nc.vector.tensor_copy
        loaded = {}
        ready = {}

        def load_wo(e):
            wo_raw = raw.tile([P, PACK, M], BF16, bufs=5)
            nc.sync.dma_start(out=wo_raw[:], in_=wo[e].rearrange("(p t) m -> p t m", t=PACK))
            loaded["wo", e] = wo_raw

        def load_h(e):
            h_raw = raw.tile([P, PACK * H], BF16, bufs=2)
            nc.sync.dma_start(out=h_raw[:], in_=h[e : e + PAIR].rearrange("e g (q j) k -> (e g q) (j k)", j=PACK))
            loaded["h", e] = h_raw

        def load_cw(first):
            g, n = divmod(first, S_TILES)
            cw_raw = raw.tile([P, PAIR, K2], BF16, bufs=6)
            nc.sync.dma_start(
                out=cw_raw[:],
                in_=combined_weights[g].rearrange("(r n) e c -> r n (e c)", n=S_TILES)[:, n : n + PAIR, :],
            )
            loaded["cw", first] = cw_raw

        def group_wo(e):
            wo_grouped = grouped.tile([P, M, PACK], BF16, align_bytes=64, name="wo_grouped")
            nc.vector.tensor_copy(
                out=wo_grouped[:].rearrange("p (c i) t -> p c t i", i=4),
                in_=loaded["wo", e][:].rearrange("p t (c i) -> p c t i", i=4),
            )
            ready["wo", e] = wo_grouped

        def quantise_wo(e):
            wo_codes = codes.tile([P, M], U32, align_bytes=64)
            wo_scales = codes.tile([P, M], U8, align_bytes=64)
            nc.vector.quantize_mx(
                out=wo_codes[:].bitcast(FP8X4),
                scales=wo_scales[:],
                in_=ready["wo", e][:].rearrange("p m t -> p (m t)"),
            )
            ready["wo", e] = (wo_codes, wo_scales)

        def turn_h(e):
            words = loaded["h", e][:].bitcast(F32)
            h_grouped = grouped.tile([P, PAIR, 2, G * C // PACK, 2 * PACK], BF16, align_bytes=64, name="h_grouped")
            for u in range(2):
                flip = banks.tile([P, 4, P], F32, tag="bank", name="h_flip")
                for n in range(2):
                    for k in range(2):
                        first = (2 * u + n) * (H // 2)
                        nc.tensor.transpose(flip[:, 2 * n + k, :], words[:, first + k : first + H // 2 : 2], ident[:])
                nc.scalar.copy(
                    out=h_grouped[:, :, u].rearrange("p e q s -> p e (q s)").bitcast(F32).rearrange("p e (q s) -> p e q s", s=4),
                    in_=flip[:].rearrange("p s (e q) -> p e q s", e=PAIR),
                )
            ready["h", e] = h_grouped

        def quantise_h(e):
            h_codes = codes.tile([P, PAIR, G * C], U32, align_bytes=64)
            h_scales = codes.tile([P, PAIR, G * C], U8, align_bytes=64)
            nc.vector.quantize_mx(
                out=h_codes[:].rearrange("p e w -> p (e w)").bitcast(FP8X4),
                scales=h_scales[:].rearrange("p e w -> p (e w)"),
                in_=ready["h", e][:].rearrange("p e u q s -> p (e u q s)"),
            )
            for i in range(PAIR):
                ready["h", e + i] = (h_codes[:, i, :], h_scales[:, i, :])

        def expert_product(e, copies):
            a, e_in = divmod(e, E_HALF)
            h_codes, h_scales = ready["h", e]
            wo_codes, wo_scales = ready["wo", e]
            for pair in range(M_CHUNKS // 2):
                eo_sum = banks.tile([P, 2, G * C], F32, tag="bank", name="eo_sum")
                for i in range(2):
                    cols = slice((2 * pair + i) * P, (2 * pair + i + 1) * P)
                    nc.tensor.matmul_mx(
                        out=eo_sum[:, i, :],
                        lhsT=wo_codes[:, cols].bitcast(FP8X4),
                        lhsT_scale=wo_scales[:, cols],
                        rhs=h_codes.bitcast(FP8X4),
                        rhs_scale=h_scales,
                        start=True,
                        stop=True,
                    )
                slots = slice(e_in * C // 2, (e_in + 1) * C // 2)
                copies[pair](
                    out=eo_turned[a][:, 2 * pair : 2 * pair + 2, :, :, slots].rearrange("p c u g w -> p (c u g) w"),
                    in_=eo_sum[:].rearrange("p c (x w) -> p (c x) w", w=C // 2),
                )

        def sort_cw(first, copy):
            cw_sorted = grouped.tile([P, PAIR, HALVES, 2, P], F32, bufs=3, name="cw_sorted")
            copy(
                out=cw_sorted[:].rearrange("p j a k w -> p (j a) w k"),
                in_=loaded["cw", first][:].rearrange("p j x -> p (j x)").bitcast(F32).rearrange("p (b w k) -> p b w k", b=PAIR * HALVES, k=2),
            )
            ready["sorted", first] = cw_sorted

        def turn_cw(first, copies, tiles=range(PAIR)):
            if 0 in tiles:
                ready["cw", first] = grouped.tile([P, PAIR, HALVES, P, PACK], BF16, align_bytes=64, bufs=4, name="cw_grouped")
            cw_grouped = ready["cw", first]
            for j in tiles:
                flip = banks.tile([P, HALVES, 2, P], F32, tag="bank", name="cw_flip")
                for a in range(HALVES):
                    for k in range(2):
                        if ("sorted", first) in ready:
                            words = ready["sorted", first][:, j, a, k, :]
                        else:
                            words = loaded["cw", first][:, j, :].bitcast(F32)[
                                :, a * K_PASS // 2 + k : (a + 1) * K_PASS // 2 : 2
                            ]
                        nc.tensor.transpose(flip[:, a, k, :], words, ident[:])
                copies[j](
                    out=cw_grouped[:, j].rearrange("p a r t -> p (a r t)").bitcast(F32).rearrange("p (a r k) -> p a r k", a=HALVES, k=2),
                    in_=flip[:].rearrange("p a k r -> p a r k"),
                )

        def quantise_cw(first):
            tiles = slice(first, first + PAIR)
            nc.vector.quantize_mx(
                out=cw_codes[:, tiles, :].rearrange("p j w -> p (j w)").bitcast(FP8X4),
                scales=cw_scales[:, tiles, :].rearrange("p j w -> p (j w)"),
                in_=ready["cw", first][:].rearrange("p j a r t -> p (j a r t)"),
            )

        def turn_eo(a, g, copies):
            eo_grouped = grouped.tile([P, M_CHUNKS, P, PACK], BF16, align_bytes=64, bufs=4, name="eo_grouped")
            for pair in range(M_CHUNKS // 2):
                flip = banks.tile([P, 2, 2, P], F32, tag="bank", name="eo_flip")
                for i in range(2):
                    for u in range(2):
                        nc.tensor.transpose(flip[:, i, u, :], eo_turned[a][:, 2 * pair + i, u, g, :].bitcast(F32), ident[:])
                copies[pair](
                    out=eo_grouped[:, 2 * pair : 2 * pair + 2].rearrange("p c m t -> p (c m t)").bitcast(F32).rearrange("p (c m u) -> p c m u", c=2, u=2),
                    in_=flip[:].rearrange("p c u m -> p c m u"),
                )
            ready["eo", a, g] = eo_grouped

        def quantise_eo(a, g):
            nc.vector.quantize_mx(
                out=eo_codes[:, g, a, :].bitcast(FP8X4),
                scales=eo_scales[:, g, a, :],
                in_=ready["eo", a, g][:].rearrange("p c m t -> p (c m t)"),
            )

        def combine(g, first):
            out_rows = out[g].rearrange("(r n) m -> r n m", n=S_TILES)
            apart = g == G - 1 and first == S_TILES - PAIR
            out_sb = result.tile([P, PAIR, M], F32)
            for j in range(PAIR):
                parts = 2 if apart and j == PAIR - 1 else 1
                for part in range(parts):
                    channels = slice(part * M // parts, (part + 1) * M // parts)
                    out_sum = banks.tile([P, M // parts], F32, tag="bank", name="out_sum")
                    for a in range(HALVES):
                        cols = slice(a * P, (a + 1) * P)
                        tile = g * S_TILES + first + j
                        nc.tensor.matmul_mx(
                            out=out_sum[:],
                            lhsT=cw_codes[:, tile, cols].bitcast(FP8X4),
                            lhsT_scale=cw_scales[:, tile, cols],
                            rhs=eo_codes[:, g, a, channels].bitcast(FP8X4),
                            rhs_scale=eo_scales[:, g, a, channels],
                            start=(a == 0),
                            stop=(a == HALVES - 1),
                        )
                    (on_scalar, on_vector)[(j + part) % 2](out=out_sb[:, j, channels], in_=out_sum[:])
                if apart:
                    nc.sync.dma_start(out=out_rows[:, first + j, :], in_=out_sb[:, j, :])
            if not apart:
                nc.sync.dma_start(out=out_rows[:, first : first + PAIR, :], in_=out_sb[:])

        SCALAR_ONLY = (on_scalar, on_scalar)
        BOTH = (on_scalar, on_vector)
        load_wo(0)
        load_h(0)
        load_wo(1)
        load_h(2)
        load_wo(2)
        load_cw(0)
        turn_h(0)
        turned = [partial(quantise_h, 0)]
        for e in range(E):
            if e + 3 < E:
                load_wo(e + 3)
            if e % 2 == 0 and e + 4 < E:
                load_h(e + 4)
            if e == 1:
                load_cw(PAIR)
            elif e % 2 == 1 and e + 1 < EARLY_TILES:
                load_cw(e + 1)
            group_wo(e)
            if e > 0:
                for quantise in turned:
                    quantise()
                turned = []
            if e == E - 1:
                turn_eo(0, 0, SCALAR_ONLY)
            elif e % 2 == 1:
                turn_h(e + 1)
                turned = [partial(quantise_h, e + 1)]
            elif e > 0:
                turn_cw(e - 2, SCALAR_ONLY)
                if e - 2 < EARLY_TILES - 4:
                    turned = [partial(quantise_cw, e - 2)]
            if e > 0:
                expert_product(e - 1, SCALAR_ONLY)
            quantise_wo(e)
        for first in range(EARLY_TILES, G * S_TILES, PAIR):
            load_cw(first)

        turn_eo(0, 1, (on_vector, on_vector))
        expert_product(E - 1, BOTH)
        turn_cw(EARLY_TILES, SCALAR_ONLY, range(1))
        quantise_eo(0, 0)
        turn_eo(1, 0, BOTH)
        turn_eo(1, 1, SCALAR_ONLY)
        quantise_eo(1, 0)
        turn_cw(EARLY_TILES, SCALAR_ONLY, range(1, PAIR))

        late = list(range(EARLY_TILES + PAIR, G * S_TILES, PAIR))
        turns = [(0, 2), (1, 2), (0, 3), (1, 3)]
        jobs = {1: [late[0], turns[0], late[1]], 4: [turns[1], late[2]], 6: [turns[2], late[3]], 8: [turns[3], late[4]], 10: [late[5], late[6]], 12: late[7:]}
        waiting = [partial(quantise_cw, first) for first in range(EARLY_TILES - 4, EARLY_TILES, PAIR)]
        waiting += [partial(quantise_eo, 0, 1), partial(quantise_eo, 1, 1), partial(quantise_cw, EARLY_TILES)]
        for i in [1,2]:
            for job in jobs.get(i, []):
                if isinstance(job, int):
                    sort_cw(job, on_vector)
        for i in range(G * S_TILES // PAIR):
            turned = []
            for job in jobs.get(i, []):
                if isinstance(job, int):
                    turn_cw(job, SCALAR_ONLY)
                    turned.append(partial(quantise_cw, job))
                else:
                    turn_eo(job[0], job[1], SCALAR_ONLY)
                    turned.append(partial(quantise_eo, job[0], job[1]))
            combine(i * PAIR // S_TILES, i * PAIR % S_TILES)
            for quantise in waiting:
                quantise()
            waiting = turned
            for job in jobs.get(i + 3, []):
                if isinstance(job, int):
                    sort_cw(job, on_vector)
